import numpy as np
import ml_dtypes


def mxq(x, axis, fmt="e4m3"):
    dtype, down = {"e4m3": (ml_dtypes.float8_e4m3fn, 7), "e5m2": (ml_dtypes.float8_e5m2, 14)}[fmt]
    v = np.moveaxis(np.asarray(x, np.float32).astype(ml_dtypes.bfloat16).astype(np.float64), axis, -1)
    blocks = v.reshape(v.shape[:-1] + (-1, 32))
    amax = np.abs(blocks).max(-1, keepdims=True)
    byte = np.maximum(np.where(amax > 0, np.frexp(amax)[1] - 1 + 127, 0) - down, 1)
    scale = np.exp2(byte - 127.0)
    codes = (blocks / scale).astype(np.float32).astype(dtype).astype(np.float64)
    return np.moveaxis((codes * scale).reshape(v.shape), -1, axis)


WIDE = False


def mx_kscale(k):
    if not WIDE:
        return np.ones(k)
    levels = np.array([10, -10, 5, -5, 0])
    if k % 512:
        return np.exp2(np.random.permutation(np.resize(levels, k // 32))).repeat(32)
    a = np.empty((k // 512, 16))
    for p in range(k // 512):
        a[p, :8] = np.random.permutation(np.resize(levels, 8))
        for g in range(8):
            far = levels[np.abs(levels - a[p, g]) >= 10]
            a[p, g + 8] = far[np.random.randint(len(far))]
    return np.exp2(a.ravel()).repeat(32)


BF16 = ml_dtypes.bfloat16


def bf(x):
    return np.asarray(x, np.float32).astype(BF16)


def f64(x):
    return np.asarray(x).astype(np.float64)


B, N, NIN, CTX, H, NOUT = 2, 512, 512, 3, 1024, 2
F = NIN * CTX


def shift_down(y, d):
    return np.pad(y[:, :-d, :], ((0, 0), (d, 0), (0, 0)))


def shift_up(y, d):
    return np.pad(y[:, d:, :], ((0, 0), (0, d), (0, 0)))


def context_linear(xq, w, shifts):
    y = xq @ mxq(w[:, :NIN].T, 0, "e4m3")
    c = 1
    for d in range(1, CTX // 2 + 1):
        for shift in shifts:
            y = y + shift(xq @ mxq(w[:, c * NIN:(c + 1) * NIN].T, 0, "e4m3"), d)
            c += 1
    return y


def setup_inputs():
    s, u = mx_kscale(NIN), mx_kscale(H)
    return {"t_bil": bf(np.random.standard_normal((B, N, NOUT, H)) * 0.15 / u),
            "x_r": bf(np.random.standard_normal((B, N, NIN)) * s),
            "W_r": bf(np.random.standard_normal((H, F)) / np.sqrt(F) / np.tile(s, CTX) * u[:, None]),
            "b_r": bf(np.random.standard_normal(H) * 0.3 * u),
            "b_bil": bf(np.random.standard_normal(NOUT))}


def reference(t_bil, x_r, W_r, b_r, b_bil):
    xq = mxq(f64(x_r), 2, "e4m3")
    hr = np.maximum(context_linear(xq, f64(W_r), (shift_up, shift_down)) + f64(b_r), 0.0)
    tq = mxq(f64(t_bil).reshape(B, N * NOUT, H), 2, "e4m3")
    sc = tq @ mxq(hr.transpose(0, 2, 1), 1, "e4m3")
    return sc.reshape(B, N, NOUT, N).transpose(0, 1, 3, 2) + f64(b_bil)

@@ -1,0 +1,232 @@
+from contextlib import ExitStack
+
+import concourse.mybir as mybir
+from concourse.masks import make_identity
+
+BF16 = mybir.dt.bfloat16
+F32 = mybir.dt.float32
+U32 = mybir.dt.uint32
+U8 = mybir.dt.uint8
+FP8X4 = mybir.dt.float8_e4m3fn_x4
+RELU = mybir.ActivationFunctionType.Relu
+IDENTITY = mybir.ActivationFunctionType.Identity
+ADD = mybir.AluOpType.add
+
+BATCH, POS, FEAT, TAPS, HID, NOUT = 2, 512, 512, 3, 1024, 2
+FLOPS = 2 * BATCH * POS * TAPS * FEAT * HID + 2 * BATCH * POS * NOUT * POS * HID
+
+P = 128
+PACK = 4
+K_PASS = P * PACK
+HALVES = 2
+PASS_WORDS = HALVES * P
+UNIT_BLOCKS = 2
+UNIT_COLS = UNIT_BLOCKS * P
+STRIDE = POS // P
+GROUPS = STRIDE + 2
+TAP_SHIFT = (0, 1, -1)
+W_TILES = HID // (2 * P)
+HID_PASSES = HID // K_PASS
+POS_TILES = POS // P
+HALF_POS = POS // 2
+
+
+def tile_bilinearpairedlayer_pb_kernel(tc, t_bil, x_r, W_r, b_r, b_bil, out):
+    nc = tc.nc
+    with ExitStack() as ctx:
+        keep = ctx.enter_context(tc.tile_pool(name="keep", bufs=1))
+        work = ctx.enter_context(tc.tile_pool(name="work", bufs=4))
+        psum = ctx.enter_context(tc.psum_pool(name="psum", bufs=8))
+
+        b_r_bf = keep.tile([P, HID_PASSES, PACK], BF16)
+        nc.scalar.dma_start(out=b_r_bf[:], in_=b_r.rearrange("(g p t) -> p g t", p=P, t=PACK))
+        b_bil_bf = keep.tile([P, NOUT], BF16)
+        nc.scalar.dma_start(out=b_bil_bf[:], in_=b_bil.partition_broadcast(P))
+
+        x_sb = [keep.tile([P, STRIDE * FEAT], BF16, name="x_sb%d" % b) for b in range(BATCH)]
+        w_sb = [keep.tile([P, 2 * TAPS * FEAT], BF16, name="w_sb%d" % a) for a in range(W_TILES)]
+        t_sb = [
+            [keep.tile([P, NOUT * HID], BF16, name="t_sb%d_%d" % (b, c)) for c in range(POS_TILES)]
+            for b in range(BATCH)
+        ]
+        w_rows = W_r.rearrange("(g p h e) c -> g h p (e c)", p=P, h=2, e=2)
+
+        def load_x(b):
+            nc.sync.dma_start(out=x_sb[b][:], in_=x_r[b].rearrange("(q r) f -> q (r f)", r=STRIDE))
+
+        load_x(0)
+        for a in range(W_TILES):
+            nc.sync.dma_start(out=w_sb[a][:], in_=w_rows[a // 2, a % 2])
+        load_x(1)
+        for b in range(BATCH):
+            t_rows = t_bil[b].rearrange("(c p) k g -> c p (k g)", p=P)
+            for c in range(POS_TILES):
+                nc.sync.dma_start(out=t_sb[b][c][:], in_=t_rows[c])
+
+        ident = keep.tile([P, P], F32)
+        make_identity(nc, ident[:])
+        bias_h = keep.tile([P, W_TILES * 2], F32)
+        nc.vector.tensor_copy(out=bias_h[:], in_=b_r_bf[:].rearrange("p g t -> p (g t)"))
+        bias_o = keep.tile([P, 2, NOUT], F32)
+        nc.vector.tensor_copy(out=bias_o[:], in_=b_bil_bf[:].unsqueeze(1).to_broadcast([P, 2, NOUT]))
+
+        x_grouped = [keep.tile([P, GROUPS * P * PACK], BF16, name="x_grouped%d" % b, align_bytes=64) for b in range(BATCH)]
+        x_codes = [keep.tile([P, GROUPS * P], U32, name="x_codes%d" % b, align_bytes=64) for b in range(BATCH)]
+        x_scales = [keep.tile([P, GROUPS * P], U8, name="x_scales%d" % b, align_bytes=64) for b in range(BATCH)]
+        w_codes = keep.tile([P, TAPS * HID], U32, align_bytes=64)
+        w_scales = keep.tile([P, TAPS * HID], U8, align_bytes=64)
+        t_codes = [keep.tile([P, NOUT * HID_PASSES * POS], U32, name="t_codes%d" % b, align_bytes=64) for b in range(BATCH)]
+        t_scales = [keep.tile([P, NOUT * HID_PASSES * POS], U8, name="t_scales%d" % b, align_bytes=64) for b in range(BATCH)]
+        h_rows = [[keep.tile([P, PACK, POS], BF16, name="h_rows%d_%d" % (b, g)) for g in range(HID_PASSES)] for b in range(BATCH)]
+        h_codes = [[keep.tile([P, POS], U32, name="h_codes%d_%d" % (b, g), align_bytes=64) for g in range(HID_PASSES)] for b in range(BATCH)]
+        h_scales = [[keep.tile([P, POS], U8, name="h_scales%d_%d" % (b, g), align_bytes=64) for g in range(HID_PASSES)] for b in range(BATCH)]
+
+        def transpose_unit(src, unit, copy, grouped):
+            words = src[:].bitcast(F32)
+            bank = psum.tile([P, HALVES, UNIT_COLS], F32, tag="bank")
+            for blk in range(UNIT_BLOCKS):
+                for u in range(HALVES):
+                    first = (unit * UNIT_BLOCKS + blk) * PASS_WORDS
+                    nc.tensor.transpose(
+                        bank[:, u, blk * P : (blk + 1) * P], words[:, first + u : first + PASS_WORDS : HALVES], ident[:]
+                    )
+            copy(
+                out=grouped.bitcast(F32).rearrange("p (c u) -> p c u", u=HALVES),
+                in_=bank[:].rearrange("p u c -> p c u"),
+            )
+
+        def quantise_tile(src, copies, codes, scales, first_col):
+            grouped = [
+                work.tile([P, UNIT_COLS * PACK], BF16, name="grouped%d" % unit, tag="grouped", bufs=6, align_bytes=64)
+                for unit in range(len(copies))
+            ]
+            for unit in range(len(copies)):
+                transpose_unit(src, unit, copies[unit], grouped[unit][:])
+            for unit in range(len(copies)):
+                cols = slice(first_col + unit * UNIT_COLS, first_col + (unit + 1) * UNIT_COLS)
+                nc.vector.quantize_mx(out=codes[:, cols].bitcast(FP8X4), scales=scales[:, cols], in_=grouped[unit][:])
+
+        def prepare_x(b):
+            grouped = x_grouped[b]
+            group = P * PACK
+            for unit in range(STRIDE // UNIT_BLOCKS):
+                first = (1 + unit * UNIT_BLOCKS) * group
+                transpose_unit(x_sb[b], unit, nc.scalar.copy, grouped[:, first : first + UNIT_BLOCKS * group])
+            nc.vector.memset(grouped[:, 0:PACK], 0.0)
+            nc.vector.memset(grouped[:, 6 * group - PACK : 6 * group], 0.0)
+            nc.vector.tensor_copy(out=grouped[:, PACK:group], in_=grouped[:, 4 * group : 5 * group - PACK])
+            nc.vector.tensor_copy(out=grouped[:, 5 * group : 6 * group - PACK], in_=grouped[:, group + PACK : 2 * group])
+            for lo, hi in ((0, 4), (4, 6)):
+                nc.vector.quantize_mx(
+                    out=x_codes[b][:, lo * P : hi * P].bitcast(FP8X4),
+                    scales=x_scales[b][:, lo * P : hi * P],
+                    in_=grouped[:, lo * group : hi * group],
+                )
+
+        def prepare_w(a):
+            copies = [nc.scalar.copy, nc.scalar.copy, nc.vector.tensor_copy]
+            quantise_tile(w_sb[a], copies, w_codes, w_scales, a * TAPS * UNIT_COLS)
+
+        def prepare_t(b, c):
+            last_copy = nc.vector.tensor_copy if c % 2 == 1 else nc.scalar.copy
+            quantise_tile(t_sb[b][c], [nc.scalar.copy, last_copy], t_codes[b], t_scales[b], c * NOUT * UNIT_COLS)
+
+        def hidden(b, a):
+            for e in range(2):
+                chunk = 2 * a + e
+                acc = psum.tile([P, POS], F32, tag="bank")
+                for tap in range(TAPS):
+                    w_cols = slice((chunk * TAPS + tap) * P, (chunk * TAPS + tap + 1) * P)
+                    x_cols = slice((1 + TAP_SHIFT[tap]) * P, (1 + TAP_SHIFT[tap]) * P + POS)
+                    nc.tensor.matmul_mx(
+                        out=acc[:],
+                        lhsT=w_codes[:, w_cols].bitcast(FP8X4),
+                        lhsT_scale=w_scales[:, w_cols],
+                        rhs=x_codes[b][:, x_cols].bitcast(FP8X4),
+                        rhs_scale=x_scales[b][:, x_cols],
+                        start=(tap == 0),
+                        stop=(tap == TAPS - 1),
+                    )
+                nc.scalar.activation(
+                    out=h_rows[b][chunk // PACK][:, chunk % PACK, :],
+                    in_=acc[:],
+                    func=RELU,
+                    bias=bias_h[:, chunk : chunk + 1],
+                    scale=1.0,
+                )
+
+        def quantise_hidden(b, g, copy):
+            grouped = work.tile([P, POS * PACK], BF16, tag="h_grouped", bufs=2, align_bytes=64)
+            for half in range(2):
+                copy(
+                    out=grouped[:, half * HALF_POS * PACK : (half + 1) * HALF_POS * PACK].rearrange(
+                        "p (c i t) -> p c t i", i=4, t=PACK
+                    ),
+                    in_=h_rows[b][g][:, :, half * HALF_POS : (half + 1) * HALF_POS].rearrange("p t (c i) -> p c t i", i=4),
+                )
+            for half in range(2):
+                cols = slice(half * HALF_POS, (half + 1) * HALF_POS)
+                nc.vector.quantize_mx(
+                    out=h_codes[b][g][:, cols].bitcast(FP8X4),
+                    scales=h_scales[b][g][:, cols],
+                    in_=grouped[:, half * HALF_POS * PACK : (half + 1) * HALF_POS * PACK],
+                )
+
+        def scores(b):
+            out_rows = out[b].rearrange("(c p) j k -> c p (j k)", p=P)
+            for c in range(POS_TILES):
+                result = work.tile([P, POS * NOUT], F32, tag="result", bufs=BATCH * POS_TILES)
+                by_group = result[:].rearrange("p (q r k) -> p q r k", r=STRIDE, k=NOUT)
+                for half in range(2):
+                    bank = psum.tile([P, NOUT, HALF_POS], F32, tag="bank")
+                    h_cols = slice(half * HALF_POS, (half + 1) * HALF_POS)
+                    for k in range(NOUT):
+                        for g in range(HID_PASSES):
+                            t_first = ((c * NOUT + k) * HID_PASSES + g) * P
+                            nc.tensor.matmul_mx(
+                                out=bank[:, k, :],
+                                lhsT=t_codes[b][:, t_first : t_first + P].bitcast(FP8X4),
+                                lhsT_scale=t_scales[b][:, t_first : t_first + P],
+                                rhs=h_codes[b][g][:, h_cols].bitcast(FP8X4),
+                                rhs_scale=h_scales[b][g][:, h_cols],
+                                start=(g == 0),
+                                stop=(g == HID_PASSES - 1),
+                            )
+                    groups = slice(2 * half, 2 * half + 2)
+                    if c == 0:
+                        for k in range(NOUT):
+                            nc.scalar.activation(
+                                out=by_group[:, :, groups, k],
+                                in_=bank[:, k, :].rearrange("p (r q) -> p q r", r=2),
+                                func=IDENTITY,
+                                bias=bias_o[:, 0, k : k + 1],
+                                scale=1.0,
+                            )
+                    else:
+                        nc.vector.tensor_tensor(
+                            out=by_group[:, :, groups, :],
+                            in0=bank[:].rearrange("p k (r q) -> p q r k", r=2),
+                            in1=bias_o[:].unsqueeze(1).to_broadcast([P, P, 2, NOUT]),
+                            op=ADD,
+                        )
+                nc.sync.dma_start(out=out_rows[c], in_=result[:])
+
+        ctx.enter_context(tc.manual_schedule())
+        prepare_x(0)
+        prepare_w(0)
+        for a in range(W_TILES):
+            if a + 1 < W_TILES:
+                prepare_w(a + 1)
+            else:
+                prepare_x(1)
+            hidden(0, a)
+            if a % 2 == 1:
+                quantise_hidden(0, a // 2, nc.vector.tensor_copy)
+        for a in range(W_TILES):
+            for t_tile in (2 * a, 2 * a + 1):
+                prepare_t(t_tile // POS_TILES, t_tile % POS_TILES)
+            hidden(1, a)
+            if a % 2 == 1:
+                quantise_hidden(1, a // 2, nc.vector.tensor_copy)
+        for b in range(BATCH):
+            scores(b)

@@ -9,7 +9,6 @@ U32 = mybir.dt.uint32
 U8 = mybir.dt.uint8
 FP8X4 = mybir.dt.float8_e4m3fn_x4
 RELU = mybir.ActivationFunctionType.Relu
-IDENTITY = mybir.ActivationFunctionType.Identity
 ADD = mybir.AluOpType.add
 
 BATCH, POS, FEAT, TAPS, HID, NOUT = 2, 512, 512, 3, 1024, 2
@@ -51,13 +50,24 @@ def tile_bilinearpairedlayer_pb_kernel(tc, t_bil, x_r, W_r, b_r, b_bil, out):
         ]
         w_rows = W_r.rearrange("(g p h e) c -> g h p (e c)", p=P, h=2, e=2)
 
-        def load_x(b):
-            nc.sync.dma_start(out=x_sb[b][:], in_=x_r[b].rearrange("(q r) f -> q (r f)", r=STRIDE))
+        def load_x(b, pieces):
+            x_rows = x_r[b].rearrange("(q r) f -> q (r f)", r=STRIDE)
+            width = STRIDE * FEAT // pieces
+            for n in range(pieces):
+                cols = slice(n * width, (n + 1) * width)
+                nc.sync.dma_start(out=x_sb[b][:, cols], in_=x_rows[:, cols])
 
-        load_x(0)
-        for a in range(W_TILES):
-            nc.sync.dma_start(out=w_sb[a][:], in_=w_rows[a // 2, a % 2])
-        load_x(1)
+        def load_w(a, pieces):
+            width = 2 * TAPS * FEAT // pieces
+            for n in range(pieces):
+                cols = slice(n * width, (n + 1) * width)
+                nc.sync.dma_start(out=w_sb[a][:, cols], in_=w_rows[a // 2, a % 2][:, cols])
+
+        load_x(0, 2)
+        load_w(0, 2)
+        for a in range(1, W_TILES):
+            load_w(a, 1)
+        load_x(1, 1)
         for b in range(BATCH):
             t_rows = t_bil[b].rearrange("(c p) k g -> c p (k g)", p=P)
             for c in range(POS_TILES):
@@ -67,8 +77,8 @@ def tile_bilinearpairedlayer_pb_kernel(tc, t_bil, x_r, W_r, b_r, b_bil, out):
         make_identity(nc, ident[:])
         bias_h = keep.tile([P, W_TILES * 2], F32)
         nc.vector.tensor_copy(out=bias_h[:], in_=b_r_bf[:].rearrange("p g t -> p (g t)"))
-        bias_o = keep.tile([P, 2, NOUT], F32)
-        nc.vector.tensor_copy(out=bias_o[:], in_=b_bil_bf[:].unsqueeze(1).to_broadcast([P, 2, NOUT]))
+        bias_o = keep.tile([P, NOUT], F32)
+        nc.vector.tensor_copy(out=bias_o[:], in_=b_bil_bf[:])
 
         x_grouped = [keep.tile([P, GROUPS * P * PACK], BF16, name="x_grouped%d" % b, align_bytes=64) for b in range(BATCH)]
         x_codes = [keep.tile([P, GROUPS * P], U32, name="x_codes%d" % b, align_bytes=64) for b in range(BATCH)]
@@ -128,8 +138,7 @@ def tile_bilinearpairedlayer_pb_kernel(tc, t_bil, x_r, W_r, b_r, b_bil, out):
             quantise_tile(w_sb[a], copies, w_codes, w_scales, a * TAPS * UNIT_COLS)
 
         def prepare_t(b, c):
-            last_copy = nc.vector.tensor_copy if c % 2 == 1 else nc.scalar.copy
-            quantise_tile(t_sb[b][c], [nc.scalar.copy, last_copy], t_codes[b], t_scales[b], c * NOUT * UNIT_COLS)
+            quantise_tile(t_sb[b][c], [nc.scalar.copy, nc.scalar.copy], t_codes[b], t_scales[b], c * NOUT * UNIT_COLS)
 
         def hidden(b, a):
             for e in range(2):
@@ -148,8 +157,8 @@ def tile_bilinearpairedlayer_pb_kernel(tc, t_bil, x_r, W_r, b_r, b_bil, out):
                         stop=(tap == TAPS - 1),
                     )
                 nc.scalar.activation(
-                    out=h_rows[b][chunk // PACK][:, chunk % PACK, :],
-                    in_=acc[:],
+                    out=h_rows[b][chunk // PACK][:, chunk % PACK, :].rearrange("p (q r) -> p q r", r=STRIDE),
+                    in_=acc[:].rearrange("p (r q) -> p q r", r=STRIDE),
                     func=RELU,
                     bias=bias_h[:, chunk : chunk + 1],
                     scale=1.0,
@@ -172,61 +181,66 @@ def tile_bilinearpairedlayer_pb_kernel(tc, t_bil, x_r, W_r, b_r, b_bil, out):
                     in_=grouped[:, half * HALF_POS * PACK : (half + 1) * HALF_POS * PACK],
                 )
 
-        def scores(b):
-            out_rows = out[b].rearrange("(c p) j k -> c p (j k)", p=P)
-            for c in range(POS_TILES):
-                result = work.tile([P, POS * NOUT], F32, tag="result", bufs=BATCH * POS_TILES)
-                by_group = result[:].rearrange("p (q r k) -> p q r k", r=STRIDE, k=NOUT)
-                for half in range(2):
-                    bank = psum.tile([P, NOUT, HALF_POS], F32, tag="bank")
-                    h_cols = slice(half * HALF_POS, (half + 1) * HALF_POS)
-                    for k in range(NOUT):
-                        for g in range(HID_PASSES):
-                            t_first = ((c * NOUT + k) * HID_PASSES + g) * P
-                            nc.tensor.matmul_mx(
-                                out=bank[:, k, :],
-                                lhsT=t_codes[b][:, t_first : t_first + P].bitcast(FP8X4),
-                                lhsT_scale=t_scales[b][:, t_first : t_first + P],
-                                rhs=h_codes[b][g][:, h_cols].bitcast(FP8X4),
-                                rhs_scale=h_scales[b][g][:, h_cols],
-                                start=(g == 0),
-                                stop=(g == HID_PASSES - 1),
-                            )
-                    groups = slice(2 * half, 2 * half + 2)
-                    if c == 0:
-                        for k in range(NOUT):
-                            nc.scalar.activation(
-                                out=by_group[:, :, groups, k],
-                                in_=bank[:, k, :].rearrange("p (r q) -> p q r", r=2),
-                                func=IDENTITY,
-                                bias=bias_o[:, 0, k : k + 1],
-                                scale=1.0,
-                            )
-                    else:
-                        nc.vector.tensor_tensor(
-                            out=by_group[:, :, groups, :],
-                            in0=bank[:].rearrange("p k (r q) -> p q r k", r=2),
-                            in1=bias_o[:].unsqueeze(1).to_broadcast([P, P, 2, NOUT]),
-                            op=ADD,
+        def scores(b, c):
+            out_rows = out[b].rearrange("(c p) j k -> c p (j k)", p=P)[c]
+            result = work.tile([P, POS * NOUT], F32, tag="result", bufs=BATCH * POS_TILES)
+            for half in range(2):
+                bank = psum.tile([P, NOUT, HALF_POS], F32, tag="bank")
+                h_cols = slice(half * HALF_POS, (half + 1) * HALF_POS)
+                for k in range(NOUT):
+                    for g in range(HID_PASSES):
+                        t_first = ((c * NOUT + k) * HID_PASSES + g) * P
+                        nc.tensor.matmul_mx(
+                            out=bank[:, k, :],
+                            lhsT=t_codes[b][:, t_first : t_first + P].bitcast(FP8X4),
+                            lhsT_scale=t_scales[b][:, t_first : t_first + P],
+                            rhs=h_codes[b][g][:, h_cols].bitcast(FP8X4),
+                            rhs_scale=h_scales[b][g][:, h_cols],
+                            start=(g == 0),
+                            stop=(g == HID_PASSES - 1),
                         )
-                nc.sync.dma_start(out=out_rows[c], in_=result[:])
+                out_cols = slice(half * HALF_POS * NOUT, (half + 1) * HALF_POS * NOUT)
+                nc.vector.tensor_tensor(
+                    out=result[:, out_cols].rearrange("p (j k) -> p j k", k=NOUT),
+                    in0=bank[:].rearrange("p k j -> p j k"),
+                    in1=bias_o[:].unsqueeze(1).to_broadcast([P, HALF_POS, NOUT]),
+                    op=ADD,
+                )
+                if b == BATCH - 1 and c == POS_TILES - 1:
+                    nc.sync.dma_start(out=out_rows[:, out_cols], in_=result[:, out_cols])
+            if not (b == BATCH - 1 and c == POS_TILES - 1):
+                nc.sync.dma_start(out=out_rows, in_=result[:])
 
         ctx.enter_context(tc.manual_schedule())
         prepare_x(0)
         prepare_w(0)
-        for a in range(W_TILES):
-            if a + 1 < W_TILES:
-                prepare_w(a + 1)
-            else:
-                prepare_x(1)
-            hidden(0, a)
-            if a % 2 == 1:
-                quantise_hidden(0, a // 2, nc.vector.tensor_copy)
-        for a in range(W_TILES):
-            for t_tile in (2 * a, 2 * a + 1):
-                prepare_t(t_tile // POS_TILES, t_tile % POS_TILES)
-            hidden(1, a)
-            if a % 2 == 1:
-                quantise_hidden(1, a // 2, nc.vector.tensor_copy)
-        for b in range(BATCH):
-            scores(b)
+        prepare_w(1)
+        hidden(0, 0)
+        prepare_w(2)
+        hidden(0, 1)
+        quantise_hidden(0, 0, nc.vector.tensor_copy)
+        prepare_w(3)
+        hidden(0, 2)
+        prepare_x(1)
+        hidden(0, 3)
+        quantise_hidden(0, 1, nc.vector.tensor_copy)
+        prepare_t(0, 0)
+        prepare_t(0, 1)
+        hidden(1, 0)
+        prepare_t(0, 2)
+        prepare_t(0, 3)
+        hidden(1, 1)
+        quantise_hidden(1, 0, nc.vector.tensor_copy)
+        scores(0, 0)
+        scores(0, 1)
+        prepare_t(1, 0)
+        prepare_t(1, 1)
+        hidden(1, 2)
+        scores(0, 2)
+        hidden(1, 3)
+        quantise_hidden(1, 1, nc.vector.tensor_copy)
+        prepare_t(1, 2)
+        prepare_t(1, 3)
+        scores(0, 3)
+        for c in range(POS_TILES):
+            scores(1, c)

@@ -75,6 +75,8 @@ def tile_bilinearpairedlayer_pb_kernel(tc, t_bil, x_r, W_r, b_r, b_bil, out):
 
         ident = keep.tile([P, P], F32)
         make_identity(nc, ident[:])
+        zeros = keep.tile([P, POS], BF16)
+        nc.vector.memset(zeros[:], 0.0)
         bias_h = keep.tile([P, W_TILES * 2], F32)
         nc.vector.tensor_copy(out=bias_h[:], in_=b_r_bf[:].rearrange("p g t -> p (g t)"))
         bias_o = keep.tile([P, NOUT], F32)
@@ -140,9 +142,8 @@ def tile_bilinearpairedlayer_pb_kernel(tc, t_bil, x_r, W_r, b_r, b_bil, out):
         def prepare_t(b, c):
             quantise_tile(t_sb[b][c], [nc.scalar.copy, nc.scalar.copy], t_codes[b], t_scales[b], c * NOUT * UNIT_COLS)
 
-        def hidden(b, a):
-            for e in range(2):
-                chunk = 2 * a + e
+        def hidden(b, *chunks):
+            for chunk in chunks:
                 acc = psum.tile([P, POS], F32, tag="bank")
                 for tap in range(TAPS):
                     w_cols = slice((chunk * TAPS + tap) * P, (chunk * TAPS + tap + 1) * P)
@@ -181,6 +182,11 @@ def tile_bilinearpairedlayer_pb_kernel(tc, t_bil, x_r, W_r, b_r, b_bil, out):
                     in_=grouped[:, half * HALF_POS * PACK : (half + 1) * HALF_POS * PACK],
                 )
 
+        def keep_clock(count):
+            bank = psum.tile([P, POS], F32, tag="bank")
+            for n in range(count):
+                nc.tensor.matmul(bank[:], zeros[:, 0:P], zeros[:], start=True, stop=True)
+
         def scores(b, c):
             out_rows = out[b].rearrange("(c p) j k -> c p (j k)", p=P)[c]
             result = work.tile([P, POS * NOUT], F32, tag="result", bufs=BATCH * POS_TILES)
@@ -212,34 +218,34 @@ def tile_bilinearpairedlayer_pb_kernel(tc, t_bil, x_r, W_r, b_r, b_bil, out):
                 nc.sync.dma_start(out=out_rows, in_=result[:])
 
         ctx.enter_context(tc.manual_schedule())
+        keep_clock(4)
         prepare_x(0)
+        keep_clock(1)
         prepare_w(0)
+        keep_clock(2)
         prepare_w(1)
-        hidden(0, 0)
+        hidden(0, 0, 1)
         prepare_w(2)
-        hidden(0, 1)
+        hidden(0, 2, 3)
         quantise_hidden(0, 0, nc.vector.tensor_copy)
         prepare_w(3)
-        hidden(0, 2)
+        hidden(0, 4, 5)
         prepare_x(1)
-        hidden(0, 3)
+        hidden(0, 6, 7)
         quantise_hidden(0, 1, nc.vector.tensor_copy)
-        prepare_t(0, 0)
-        prepare_t(0, 1)
-        hidden(1, 0)
-        prepare_t(0, 2)
-        prepare_t(0, 3)
-        hidden(1, 1)
+        for c in range(POS_TILES):
+            prepare_t(0, c)
+            hidden(1, c)
         quantise_hidden(1, 0, nc.vector.tensor_copy)
         scores(0, 0)
-        scores(0, 1)
         prepare_t(1, 0)
+        scores(0, 1)
         prepare_t(1, 1)
-        hidden(1, 2)
-        scores(0, 2)
-        hidden(1, 3)
-        quantise_hidden(1, 1, nc.vector.tensor_copy)
+        hidden(1, 4, 5)
         prepare_t(1, 2)
+        scores(0, 2)
+        hidden(1, 6, 7)
+        quantise_hidden(1, 1, nc.vector.tensor_copy)
         prepare_t(1, 3)
         scores(0, 3)
         for c in range(POS_TILES):

@@ -9,6 +9,7 @@ U32 = mybir.dt.uint32
 U8 = mybir.dt.uint8
 FP8X4 = mybir.dt.float8_e4m3fn_x4
 RELU = mybir.ActivationFunctionType.Relu
+IDENTITY = mybir.ActivationFunctionType.Identity
 ADD = mybir.AluOpType.add
 
 BATCH, POS, FEAT, TAPS, HID, NOUT = 2, 512, 512, 3, 1024, 2
@@ -93,37 +94,49 @@ def tile_bilinearpairedlayer_pb_kernel(tc, t_bil, x_r, W_r, b_r, b_bil, out):
         h_codes = [[keep.tile([P, POS], U32, name="h_codes%d_%d" % (b, g), align_bytes=64) for g in range(HID_PASSES)] for b in range(BATCH)]
         h_scales = [[keep.tile([P, POS], U8, name="h_scales%d_%d" % (b, g), align_bytes=64) for g in range(HID_PASSES)] for b in range(BATCH)]
 
-        def transpose_unit(src, unit, copy, grouped):
-            words = src[:].bitcast(F32)
+        def sort_words(src, tag, bufs):
+            in_order = work.tile([P, src[:].shape[1] // 2], F32, name="in_order_" + tag, tag="in_order_" + tag, bufs=bufs)
+            nc.vector.tensor_copy(
+                out=in_order[:].rearrange("p (n u w) -> p n u w", u=HALVES, w=P),
+                in_=src[:].bitcast(F32).rearrange("p (n w u) -> p n u w", u=HALVES, w=P),
+            )
+            return in_order
+
+        def transpose_unit(words, is_sorted, unit, copy, grouped):
             bank = psum.tile([P, HALVES, UNIT_COLS], F32, tag="bank")
             for blk in range(UNIT_BLOCKS):
+                first = (unit * UNIT_BLOCKS + blk) * PASS_WORDS
                 for u in range(HALVES):
-                    first = (unit * UNIT_BLOCKS + blk) * PASS_WORDS
-                    nc.tensor.transpose(
-                        bank[:, u, blk * P : (blk + 1) * P], words[:, first + u : first + PASS_WORDS : HALVES], ident[:]
-                    )
+                    if is_sorted:
+                        half = words[:, first + u * P : first + (u + 1) * P]
+                    else:
+                        half = words[:, first + u : first + PASS_WORDS : HALVES]
+                    nc.tensor.transpose(bank[:, u, blk * P : (blk + 1) * P], half, ident[:])
             copy(
                 out=grouped.bitcast(F32).rearrange("p (c u) -> p c u", u=HALVES),
                 in_=bank[:].rearrange("p u c -> p c u"),
             )
 
-        def quantise_tile(src, copies, codes, scales, first_col):
+        def transpose_tile(words, is_sorted, copies):
             grouped = [
-                work.tile([P, UNIT_COLS * PACK], BF16, name="grouped%d" % unit, tag="grouped", bufs=6, align_bytes=64)
+                work.tile([P, UNIT_COLS * PACK], BF16, name="grouped%d" % unit, tag="grouped", bufs=8, align_bytes=64)
                 for unit in range(len(copies))
             ]
             for unit in range(len(copies)):
-                transpose_unit(src, unit, copies[unit], grouped[unit][:])
-            for unit in range(len(copies)):
+                transpose_unit(words, is_sorted, unit, copies[unit], grouped[unit][:])
+            return grouped
+
+        def quantise_tile(grouped, codes, scales, first_col):
+            for unit in range(len(grouped)):
                 cols = slice(first_col + unit * UNIT_COLS, first_col + (unit + 1) * UNIT_COLS)
                 nc.vector.quantize_mx(out=codes[:, cols].bitcast(FP8X4), scales=scales[:, cols], in_=grouped[unit][:])
 
-        def prepare_x(b):
+        def prepare_x(b, words, is_sorted):
             grouped = x_grouped[b]
             group = P * PACK
             for unit in range(STRIDE // UNIT_BLOCKS):
                 first = (1 + unit * UNIT_BLOCKS) * group
-                transpose_unit(x_sb[b], unit, nc.scalar.copy, grouped[:, first : first + UNIT_BLOCKS * group])
+                transpose_unit(words, is_sorted, unit, nc.scalar.copy, grouped[:, first : first + UNIT_BLOCKS * group])
             nc.vector.memset(grouped[:, 0:PACK], 0.0)
             nc.vector.memset(grouped[:, 6 * group - PACK : 6 * group], 0.0)
             nc.vector.tensor_copy(out=grouped[:, PACK:group], in_=grouped[:, 4 * group : 5 * group - PACK])
@@ -135,12 +148,12 @@ def tile_bilinearpairedlayer_pb_kernel(tc, t_bil, x_r, W_r, b_r, b_bil, out):
                     in_=grouped[:, lo * group : hi * group],
                 )
 
-        def prepare_w(a):
-            copies = [nc.scalar.copy, nc.scalar.copy, nc.vector.tensor_copy]
-            quantise_tile(w_sb[a], copies, w_codes, w_scales, a * TAPS * UNIT_COLS)
+        def prepare_w(a, words, is_sorted):
+            grouped = transpose_tile(words, is_sorted, [nc.scalar.copy] * 3)
+            quantise_tile(grouped, w_codes, w_scales, a * TAPS * UNIT_COLS)
 
-        def prepare_t(b, c):
-            quantise_tile(t_sb[b][c], [nc.scalar.copy, nc.scalar.copy], t_codes[b], t_scales[b], c * NOUT * UNIT_COLS)
+        def quantise_t(b, c, grouped):
+            quantise_tile(grouped, t_codes[b], t_scales[b], c * NOUT * UNIT_COLS)
 
         def hidden(b, *chunks):
             for chunk in chunks:
@@ -187,9 +200,9 @@ def tile_bilinearpairedlayer_pb_kernel(tc, t_bil, x_r, W_r, b_r, b_bil, out):
             for n in range(count):
                 nc.tensor.matmul(bank[:], zeros[:, 0:P], zeros[:], start=True, stop=True)
 
-        def scores(b, c):
+        def scores(b, c, engines="VV"):
             out_rows = out[b].rearrange("(c p) j k -> c p (j k)", p=P)[c]
-            result = work.tile([P, POS * NOUT], F32, tag="result", bufs=BATCH * POS_TILES)
+            result = work.tile([P, POS * NOUT], F32, tag="result", bufs=6)
             for half in range(2):
                 bank = psum.tile([P, NOUT, HALF_POS], F32, tag="bank")
                 h_cols = slice(half * HALF_POS, (half + 1) * HALF_POS)
@@ -206,47 +219,89 @@ def tile_bilinearpairedlayer_pb_kernel(tc, t_bil, x_r, W_r, b_r, b_bil, out):
                             stop=(g == HID_PASSES - 1),
                         )
                 out_cols = slice(half * HALF_POS * NOUT, (half + 1) * HALF_POS * NOUT)
-                nc.vector.tensor_tensor(
-                    out=result[:, out_cols].rearrange("p (j k) -> p j k", k=NOUT),
-                    in0=bank[:].rearrange("p k j -> p j k"),
-                    in1=bias_o[:].unsqueeze(1).to_broadcast([P, HALF_POS, NOUT]),
-                    op=ADD,
-                )
+                by_k = result[:, out_cols].rearrange("p (j k) -> p j k", k=NOUT)
+                if engines[half] == "V":
+                    nc.vector.tensor_tensor(
+                        out=by_k,
+                        in0=bank[:].rearrange("p k j -> p j k"),
+                        in1=bias_o[:].unsqueeze(1).to_broadcast([P, HALF_POS, NOUT]),
+                        op=ADD,
+                    )
+                else:
+                    for k in range(NOUT):
+                        nc.scalar.activation(
+                            out=by_k[:, :, k], in_=bank[:, k, :], func=IDENTITY, bias=bias_o[:, k : k + 1], scale=1.0
+                        )
                 if b == BATCH - 1 and c == POS_TILES - 1:
                     nc.sync.dma_start(out=out_rows[:, out_cols], in_=result[:, out_cols])
             if not (b == BATCH - 1 and c == POS_TILES - 1):
                 nc.sync.dma_start(out=out_rows, in_=result[:])
 
         ctx.enter_context(tc.manual_schedule())
+        in_order = {}
+        grouped = {}
+
+        def sort_t(b, c):
+            in_order[b, c] = sort_words(t_sb[b][c], "t", 4)
+
+        def transpose_t(b, c):
+            is_sorted = (b, c) in in_order
+            words = in_order[b, c] if is_sorted else t_sb[b][c][:].bitcast(F32)
+            grouped[b, c] = transpose_tile(words, is_sorted, [nc.scalar.copy] * 2)
+
         keep_clock(4)
-        prepare_x(0)
+        prepare_x(0, x_sb[0][:].bitcast(F32), False)
         keep_clock(1)
-        prepare_w(0)
+        prepare_w(0, w_sb[0][:].bitcast(F32), False)
+        w2 = sort_words(w_sb[2], "w", 2)
         keep_clock(2)
-        prepare_w(1)
+        prepare_w(1, w_sb[1][:].bitcast(F32), False)
         hidden(0, 0, 1)
-        prepare_w(2)
+        w3 = sort_words(w_sb[3], "w", 2)
+        prepare_w(2, w2, True)
         hidden(0, 2, 3)
-        quantise_hidden(0, 0, nc.vector.tensor_copy)
-        prepare_w(3)
+        x1 = sort_words(x_sb[1], "x", 1)
+        prepare_w(3, w3, True)
         hidden(0, 4, 5)
-        prepare_x(1)
+        sort_t(0, 0)
+        prepare_x(1, x1, True)
+        sort_t(0, 1)
+        quantise_hidden(0, 0, nc.vector.tensor_copy)
         hidden(0, 6, 7)
+        sort_t(0, 2)
+        transpose_t(0, 0)
+        hidden(1, 0)
+        sort_t(0, 3)
         quantise_hidden(0, 1, nc.vector.tensor_copy)
-        for c in range(POS_TILES):
-            prepare_t(0, c)
-            hidden(1, c)
-        quantise_hidden(1, 0, nc.vector.tensor_copy)
+        transpose_t(0, 1)
+        hidden(1, 1)
+        quantise_t(0, 0, grouped[0, 0])
+        sort_t(1, 0)
+        transpose_t(0, 2)
+        hidden(1, 2)
+        quantise_t(0, 1, grouped[0, 1])
+        sort_t(1, 1)
+        transpose_t(0, 3)
+        hidden(1, 3)
+        quantise_t(0, 2, grouped[0, 2])
         scores(0, 0)
-        prepare_t(1, 0)
+        transpose_t(1, 0)
+        quantise_t(0, 3, grouped[0, 3])
+        quantise_hidden(1, 0, nc.vector.tensor_copy)
         scores(0, 1)
-        prepare_t(1, 1)
+        transpose_t(1, 1)
+        quantise_t(1, 0, grouped[1, 0])
         hidden(1, 4, 5)
-        prepare_t(1, 2)
+        transpose_t(1, 2)
+        quantise_t(1, 1, grouped[1, 1])
         scores(0, 2)
         hidden(1, 6, 7)
+        transpose_t(1, 3)
+        quantise_t(1, 2, grouped[1, 2])
         quantise_hidden(1, 1, nc.vector.tensor_copy)
-        prepare_t(1, 3)
-        scores(0, 3)
-        for c in range(POS_TILES):
-            scores(1, c)
+        scores(0, 3, "VS")
+        scores(1, 0, "SV")
+        quantise_t(1, 3, grouped[1, 3])
+        scores(1, 1, "SV")
+        scores(1, 2)
+        scores(1, 3)

@@ -13,6 +13,7 @@ IDENTITY = mybir.ActivationFunctionType.Identity
 ADD = mybir.AluOpType.add
 
 BATCH, POS, FEAT, TAPS, HID, NOUT = 2, 512, 512, 3, 1024, 2
+GROUPED_BUFS = {2: 4, 3: 2}
 FLOPS = 2 * BATCH * POS * TAPS * FEAT * HID + 2 * BATCH * POS * NOUT * POS * HID
 
 P = 128
@@ -117,26 +118,30 @@ def tile_bilinearpairedlayer_pb_kernel(tc, t_bil, x_r, W_r, b_r, b_bil, out):
                 in_=bank[:].rearrange("p u c -> p c u"),
             )
 
-        def transpose_tile(words, is_sorted, copies):
-            grouped = [
-                work.tile([P, UNIT_COLS * PACK], BF16, name="grouped%d" % unit, tag="grouped", bufs=8, align_bytes=64)
-                for unit in range(len(copies))
-            ]
-            for unit in range(len(copies)):
-                transpose_unit(words, is_sorted, unit, copies[unit], grouped[unit][:])
+        def transpose_tile(words, is_sorted, units):
+            unit_elems = UNIT_COLS * PACK
+            grouped = work.tile([P, units * unit_elems], BF16, name="grouped%d" % units, tag="grouped%d" % units, bufs=GROUPED_BUFS[units], align_bytes=64)
+            for unit in range(units):
+                transpose_unit(words, is_sorted, unit, nc.scalar.copy, grouped[:, unit * unit_elems : (unit + 1) * unit_elems])
             return grouped
 
-        def quantise_tile(grouped, codes, scales, first_col):
-            for unit in range(len(grouped)):
-                cols = slice(first_col + unit * UNIT_COLS, first_col + (unit + 1) * UNIT_COLS)
-                nc.vector.quantize_mx(out=codes[:, cols].bitcast(FP8X4), scales=scales[:, cols], in_=grouped[unit][:])
+        def quantise_units(grouped, codes, scales, first_col, lo, hi):
+            cols = slice(first_col + lo * UNIT_COLS, first_col + hi * UNIT_COLS)
+            nc.vector.quantize_mx(
+                out=codes[:, cols].bitcast(FP8X4),
+                scales=scales[:, cols],
+                in_=grouped[:, lo * UNIT_COLS * PACK : hi * UNIT_COLS * PACK],
+            )
 
-        def prepare_x(b, words, is_sorted):
-            grouped = x_grouped[b]
+        def transpose_x(b, words, is_sorted):
             group = P * PACK
             for unit in range(STRIDE // UNIT_BLOCKS):
                 first = (1 + unit * UNIT_BLOCKS) * group
-                transpose_unit(words, is_sorted, unit, nc.scalar.copy, grouped[:, first : first + UNIT_BLOCKS * group])
+                transpose_unit(words, is_sorted, unit, nc.scalar.copy, x_grouped[b][:, first : first + UNIT_BLOCKS * group])
+
+        def quantise_x(b):
+            grouped = x_grouped[b]
+            group = P * PACK
             nc.vector.memset(grouped[:, 0:PACK], 0.0)
             nc.vector.memset(grouped[:, 6 * group - PACK : 6 * group], 0.0)
             nc.vector.tensor_copy(out=grouped[:, PACK:group], in_=grouped[:, 4 * group : 5 * group - PACK])
@@ -148,12 +153,12 @@ def tile_bilinearpairedlayer_pb_kernel(tc, t_bil, x_r, W_r, b_r, b_bil, out):
                     in_=grouped[:, lo * group : hi * group],
                 )
 
-        def prepare_w(a, words, is_sorted):
-            grouped = transpose_tile(words, is_sorted, [nc.scalar.copy] * 3)
-            quantise_tile(grouped, w_codes, w_scales, a * TAPS * UNIT_COLS)
+        def quantise_w(a, grouped):
+            for lo, hi in ((0, 2), (2, 3)):
+                quantise_units(grouped, w_codes, w_scales, a * TAPS * UNIT_COLS, lo, hi)
 
         def quantise_t(b, c, grouped):
-            quantise_tile(grouped, t_codes[b], t_scales[b], c * NOUT * UNIT_COLS)
+            quantise_units(grouped, t_codes[b], t_scales[b], c * NOUT * UNIT_COLS, 0, 2)
 
         def hidden(b, *chunks):
             for chunk in chunks:
@@ -178,10 +183,10 @@ def tile_bilinearpairedlayer_pb_kernel(tc, t_bil, x_r, W_r, b_r, b_bil, out):
                     scale=1.0,
                 )
 
-        def quantise_hidden(b, g, copy):
+        def quantise_hidden(b, g, copies):
             grouped = work.tile([P, POS * PACK], BF16, tag="h_grouped", bufs=2, align_bytes=64)
             for half in range(2):
-                copy(
+                copies[half](
                     out=grouped[:, half * HALF_POS * PACK : (half + 1) * HALF_POS * PACK].rearrange(
                         "p (c i t) -> p c t i", i=4, t=PACK
                     ),
@@ -202,7 +207,7 @@ def tile_bilinearpairedlayer_pb_kernel(tc, t_bil, x_r, W_r, b_r, b_bil, out):
 
         def scores(b, c, engines="VV"):
             out_rows = out[b].rearrange("(c p) j k -> c p (j k)", p=P)[c]
-            result = work.tile([P, POS * NOUT], F32, tag="result", bufs=6)
+            result = work.tile([P, POS * NOUT], F32, tag="result", bufs=5)
             for half in range(2):
                 bank = psum.tile([P, NOUT, HALF_POS], F32, tag="bank")
                 h_cols = slice(half * HALF_POS, (half + 1) * HALF_POS)
@@ -245,60 +250,67 @@ def tile_bilinearpairedlayer_pb_kernel(tc, t_bil, x_r, W_r, b_r, b_bil, out):
             in_order[b, c] = sort_words(t_sb[b][c], "t", 4)
 
         def transpose_t(b, c):
-            is_sorted = (b, c) in in_order
-            words = in_order[b, c] if is_sorted else t_sb[b][c][:].bitcast(F32)
-            grouped[b, c] = transpose_tile(words, is_sorted, [nc.scalar.copy] * 2)
+            grouped[b, c] = transpose_tile(in_order[b, c], True, 2)
+
+        on_vector = [nc.vector.tensor_copy, nc.vector.tensor_copy]
+        shared = [nc.vector.tensor_copy, nc.scalar.copy]
 
         keep_clock(4)
-        prepare_x(0, x_sb[0][:].bitcast(F32), False)
+        transpose_x(0, x_sb[0][:].bitcast(F32), False)
         keep_clock(1)
-        prepare_w(0, w_sb[0][:].bitcast(F32), False)
-        w2 = sort_words(w_sb[2], "w", 2)
+        w0 = transpose_tile(w_sb[0][:].bitcast(F32), False, 3)
+        quantise_x(0)
+        quantise_w(0, w0)
         keep_clock(2)
-        prepare_w(1, w_sb[1][:].bitcast(F32), False)
+        w1 = transpose_tile(w_sb[1][:].bitcast(F32), False, 3)
+        in_order_w2 = sort_words(w_sb[2], "w", 2)
+        quantise_w(1, w1)
         hidden(0, 0, 1)
-        w3 = sort_words(w_sb[3], "w", 2)
-        prepare_w(2, w2, True)
+        w2 = transpose_tile(in_order_w2, True, 3)
+        in_order_w3 = sort_words(w_sb[3], "w", 2)
+        quantise_w(2, w2)
         hidden(0, 2, 3)
-        x1 = sort_words(x_sb[1], "x", 1)
-        prepare_w(3, w3, True)
-        hidden(0, 4, 5)
+        in_order_x1 = sort_words(x_sb[1], "t", 4)
+        w3 = transpose_tile(in_order_w3, True, 3)
+        quantise_w(3, w3)
         sort_t(0, 0)
-        prepare_x(1, x1, True)
+        hidden(0, 4, 5)
+        transpose_x(1, in_order_x1, True)
         sort_t(0, 1)
-        quantise_hidden(0, 0, nc.vector.tensor_copy)
-        hidden(0, 6, 7)
+        quantise_x(1)
+        quantise_hidden(0, 0, shared)
         sort_t(0, 2)
+        hidden(0, 6, 7)
         transpose_t(0, 0)
-        hidden(1, 0)
-        sort_t(0, 3)
-        quantise_hidden(0, 1, nc.vector.tensor_copy)
         transpose_t(0, 1)
-        hidden(1, 1)
+        sort_t(0, 3)
         quantise_t(0, 0, grouped[0, 0])
+        hidden(1, 0, 1)
         sort_t(1, 0)
-        transpose_t(0, 2)
-        hidden(1, 2)
         quantise_t(0, 1, grouped[0, 1])
-        sort_t(1, 1)
+        quantise_hidden(0, 1, shared)
+        transpose_t(0, 2)
         transpose_t(0, 3)
-        hidden(1, 3)
+        sort_t(1, 1)
         quantise_t(0, 2, grouped[0, 2])
-        scores(0, 0)
-        transpose_t(1, 0)
+        hidden(1, 2, 3)
         quantise_t(0, 3, grouped[0, 3])
-        quantise_hidden(1, 0, nc.vector.tensor_copy)
+        scores(0, 0)
         scores(0, 1)
+        sort_t(1, 2)
+        quantise_hidden(1, 0, shared)
+        transpose_t(1, 0)
         transpose_t(1, 1)
+        sort_t(1, 3)
         quantise_t(1, 0, grouped[1, 0])
         hidden(1, 4, 5)
-        transpose_t(1, 2)
         quantise_t(1, 1, grouped[1, 1])
         scores(0, 2)
         hidden(1, 6, 7)
+        transpose_t(1, 2)
         transpose_t(1, 3)
+        quantise_hidden(1, 1, on_vector)
         quantise_t(1, 2, grouped[1, 2])
-        quantise_hidden(1, 1, nc.vector.tensor_copy)
         scores(0, 3, "VS")
         scores(1, 0, "SV")
         quantise_t(1, 3, grouped[1, 3])

@@ -67,9 +67,9 @@ def tile_bilinearpairedlayer_pb_kernel(tc, t_bil, x_r, W_r, b_r, b_bil, out):
 
         load_x(0, 2)
         load_w(0, 2)
+        load_x(1, 1)
         for a in range(1, W_TILES):
             load_w(a, 1)
-        load_x(1, 1)
         for b in range(BATCH):
             t_rows = t_bil[b].rearrange("(c p) k g -> c p (k g)", p=P)
             for c in range(POS_TILES):
@@ -207,7 +207,7 @@ def tile_bilinearpairedlayer_pb_kernel(tc, t_bil, x_r, W_r, b_r, b_bil, out):
 
         def scores(b, c, engines="VV"):
             out_rows = out[b].rearrange("(c p) j k -> c p (j k)", p=P)[c]
-            result = work.tile([P, POS * NOUT], F32, tag="result", bufs=5)
+            result = work.tile([P, POS * NOUT], F32, tag="result", bufs=6)
             for half in range(2):
                 bank = psum.tile([P, NOUT, HALF_POS], F32, tag="bank")
                 h_cols = slice(half * HALF_POS, (half + 1) * HALF_POS)
@@ -250,10 +250,11 @@ def tile_bilinearpairedlayer_pb_kernel(tc, t_bil, x_r, W_r, b_r, b_bil, out):
             in_order[b, c] = sort_words(t_sb[b][c], "t", 4)
 
         def transpose_t(b, c):
-            grouped[b, c] = transpose_tile(in_order[b, c], True, 2)
+            is_sorted = (b, c) in in_order
+            words = in_order[b, c] if is_sorted else t_sb[b][c][:].bitcast(F32)
+            grouped[b, c] = transpose_tile(words, is_sorted, 2)
 
         on_vector = [nc.vector.tensor_copy, nc.vector.tensor_copy]
-        shared = [nc.vector.tensor_copy, nc.scalar.copy]
 
         keep_clock(4)
         transpose_x(0, x_sb[0][:].bitcast(F32), False)
@@ -261,59 +262,57 @@ def tile_bilinearpairedlayer_pb_kernel(tc, t_bil, x_r, W_r, b_r, b_bil, out):
         w0 = transpose_tile(w_sb[0][:].bitcast(F32), False, 3)
         quantise_x(0)
         quantise_w(0, w0)
-        keep_clock(2)
+        keep_clock(1)
+        transpose_x(1, x_sb[1][:].bitcast(F32), False)
+        keep_clock(1)
         w1 = transpose_tile(w_sb[1][:].bitcast(F32), False, 3)
-        in_order_w2 = sort_words(w_sb[2], "w", 2)
-        quantise_w(1, w1)
-        hidden(0, 0, 1)
-        w2 = transpose_tile(in_order_w2, True, 3)
-        in_order_w3 = sort_words(w_sb[3], "w", 2)
-        quantise_w(2, w2)
-        hidden(0, 2, 3)
-        in_order_x1 = sort_words(x_sb[1], "t", 4)
-        w3 = transpose_tile(in_order_w3, True, 3)
-        quantise_w(3, w3)
-        sort_t(0, 0)
-        hidden(0, 4, 5)
-        transpose_x(1, in_order_x1, True)
-        sort_t(0, 1)
         quantise_x(1)
-        quantise_hidden(0, 0, shared)
+        quantise_w(1, w1)
+        sorted_w2 = sort_words(w_sb[2], "w", 2)
+        hidden(0, 0, 1)
+        hidden(1, 0, 1)
+        sorted_w3 = sort_words(w_sb[3], "w", 2)
+        w2 = transpose_tile(sorted_w2, True, 3)
+        hidden(0, 2, 3)
+        hidden(1, 2, 3)
+        sort_t(0, 0)
+        w3 = transpose_tile(sorted_w3, True, 3)
+        quantise_w(2, w2)
+        sort_t(0, 1)
+        quantise_hidden(0, 0, on_vector)
+        quantise_w(3, w3)
+        hidden(0, 4, 5)
+        hidden(1, 4, 5)
         sort_t(0, 2)
-        hidden(0, 6, 7)
         transpose_t(0, 0)
         transpose_t(0, 1)
+        quantise_hidden(1, 0, on_vector)
         sort_t(0, 3)
+        hidden(0, 6, 7)
         quantise_t(0, 0, grouped[0, 0])
-        hidden(1, 0, 1)
-        sort_t(1, 0)
-        quantise_t(0, 1, grouped[0, 1])
-        quantise_hidden(0, 1, shared)
         transpose_t(0, 2)
         transpose_t(0, 3)
+        sort_t(1, 0)
         sort_t(1, 1)
-        quantise_t(0, 2, grouped[0, 2])
-        hidden(1, 2, 3)
-        quantise_t(0, 3, grouped[0, 3])
-        scores(0, 0)
-        scores(0, 1)
-        sort_t(1, 2)
-        quantise_hidden(1, 0, shared)
+        quantise_t(0, 1, grouped[0, 1])
+        hidden(1, 6, 7)
+        quantise_hidden(0, 1, on_vector)
         transpose_t(1, 0)
         transpose_t(1, 1)
-        sort_t(1, 3)
-        quantise_t(1, 0, grouped[1, 0])
-        hidden(1, 4, 5)
-        quantise_t(1, 1, grouped[1, 1])
-        scores(0, 2)
-        hidden(1, 6, 7)
-        transpose_t(1, 2)
-        transpose_t(1, 3)
+        quantise_t(0, 2, grouped[0, 2])
+        scores(0, 0, "VS")
+        quantise_t(0, 3, grouped[0, 3])
         quantise_hidden(1, 1, on_vector)
+        scores(0, 1, "VS")
+        scores(0, 2, "VS")
+        quantise_t(1, 0, grouped[1, 0])
+        transpose_t(1, 2)
+        quantise_t(1, 1, grouped[1, 1])
+        scores(0, 3)
+        transpose_t(1, 3)
+        scores(1, 0, "VS")
         quantise_t(1, 2, grouped[1, 2])
-        scores(0, 3, "VS")
-        scores(1, 0, "SV")
+        scores(1, 1)
         quantise_t(1, 3, grouped[1, 3])
-        scores(1, 1, "SV")
         scores(1, 2)
         scores(1, 3)

@@ -40,9 +40,7 @@ def tile_bilinearpairedlayer_pb_kernel(tc, t_bil, x_r, W_r, b_r, b_bil, out):
         psum = ctx.enter_context(tc.psum_pool(name="psum", bufs=8))
 
         b_r_bf = keep.tile([P, HID_PASSES, PACK], BF16)
-        nc.scalar.dma_start(out=b_r_bf[:], in_=b_r.rearrange("(g p t) -> p g t", p=P, t=PACK))
         b_bil_bf = keep.tile([P, NOUT], BF16)
-        nc.scalar.dma_start(out=b_bil_bf[:], in_=b_bil.partition_broadcast(P))
 
         x_sb = [keep.tile([P, STRIDE * FEAT], BF16, name="x_sb%d" % b) for b in range(BATCH)]
         w_sb = [keep.tile([P, 2 * TAPS * FEAT], BF16, name="w_sb%d" % a) for a in range(W_TILES)]
@@ -68,6 +66,7 @@ def tile_bilinearpairedlayer_pb_kernel(tc, t_bil, x_r, W_r, b_r, b_bil, out):
         load_x(0, 2)
         load_w(0, 2)
         load_x(1, 1)
+        nc.sync.dma_start(out=b_r_bf[:], in_=b_r.rearrange("(g p t) -> p g t", p=P, t=PACK))
         for a in range(1, W_TILES):
             load_w(a, 1)
         for b in range(BATCH):
@@ -75,14 +74,12 @@ def tile_bilinearpairedlayer_pb_kernel(tc, t_bil, x_r, W_r, b_r, b_bil, out):
             for c in range(POS_TILES):
                 nc.sync.dma_start(out=t_sb[b][c][:], in_=t_rows[c])
 
+        nc.sync.dma_start(out=b_bil_bf[:], in_=b_bil.partition_broadcast(P))
+
         ident = keep.tile([P, P], F32)
         make_identity(nc, ident[:])
         zeros = keep.tile([P, POS], BF16)
         nc.vector.memset(zeros[:], 0.0)
-        bias_h = keep.tile([P, W_TILES * 2], F32)
-        nc.vector.tensor_copy(out=bias_h[:], in_=b_r_bf[:].rearrange("p g t -> p (g t)"))
-        bias_o = keep.tile([P, NOUT], F32)
-        nc.vector.tensor_copy(out=bias_o[:], in_=b_bil_bf[:])
 
         x_grouped = [keep.tile([P, GROUPS * P * PACK], BF16, name="x_grouped%d" % b, align_bytes=64) for b in range(BATCH)]
         x_codes = [keep.tile([P, GROUPS * P], U32, name="x_codes%d" % b, align_bytes=64) for b in range(BATCH)]
@@ -179,7 +176,7 @@ def tile_bilinearpairedlayer_pb_kernel(tc, t_bil, x_r, W_r, b_r, b_bil, out):
                     out=h_rows[b][chunk // PACK][:, chunk % PACK, :].rearrange("p (q r) -> p q r", r=STRIDE),
                     in_=acc[:].rearrange("p (r q) -> p q r", r=STRIDE),
                     func=RELU,
-                    bias=bias_h[:, chunk : chunk + 1],
+                    bias=b_r_bf[:, chunk // PACK, chunk % PACK : chunk % PACK + 1],
                     scale=1.0,
                 )
 
@@ -229,13 +226,13 @@ def tile_bilinearpairedlayer_pb_kernel(tc, t_bil, x_r, W_r, b_r, b_bil, out):
                     nc.vector.tensor_tensor(
                         out=by_k,
                         in0=bank[:].rearrange("p k j -> p j k"),
-                        in1=bias_o[:].unsqueeze(1).to_broadcast([P, HALF_POS, NOUT]),
+                        in1=b_bil_bf[:].unsqueeze(1).to_broadcast([P, HALF_POS, NOUT]),
                         op=ADD,
                     )
                 else:
                     for k in range(NOUT):
                         nc.scalar.activation(
-                            out=by_k[:, :, k], in_=bank[:, k, :], func=IDENTITY, bias=bias_o[:, k : k + 1], scale=1.0
+                            out=by_k[:, :, k], in_=bank[:, k, :], func=IDENTITY, bias=b_bil_bf[:, k : k + 1], scale=1.0
                         )
                 if b == BATCH - 1 and c == POS_TILES - 1:
                     nc.sync.dma_start(out=out_rows[:, out_cols], in_=result[:, out_cols])

@@ -203,6 +203,7 @@ def tile_bilinearpairedlayer_pb_kernel(tc, t_bil, x_r, W_r, b_r, b_bil, out):
                 nc.tensor.matmul(bank[:], zeros[:, 0:P], zeros[:], start=True, stop=True)
 
         def scores(b, c, engines="VV"):
+            by_halves = engines != "VV" or (b == BATCH - 1 and c == POS_TILES - 1)
             out_rows = out[b].rearrange("(c p) j k -> c p (j k)", p=P)[c]
             result = work.tile([P, POS * NOUT], F32, tag="result", bufs=6)
             for half in range(2):
@@ -234,9 +235,10 @@ def tile_bilinearpairedlayer_pb_kernel(tc, t_bil, x_r, W_r, b_r, b_bil, out):
                         nc.scalar.activation(
                             out=by_k[:, :, k], in_=bank[:, k, :], func=IDENTITY, bias=b_bil_bf[:, k : k + 1], scale=1.0
                         )
-                if b == BATCH - 1 and c == POS_TILES - 1:
-                    nc.sync.dma_start(out=out_rows[:, out_cols], in_=result[:, out_cols])
-            if not (b == BATCH - 1 and c == POS_TILES - 1):
+                if by_halves:
+                    queue = nc.scalar if engines[half] == "S" else nc.sync
+                    queue.dma_start(out=out_rows[:, out_cols], in_=result[:, out_cols])
+            if not by_halves:
                 nc.sync.dma_start(out=out_rows, in_=result[:])
 
         ctx.enter_context(tc.manual_schedule())
@@ -255,13 +257,10 @@ def tile_bilinearpairedlayer_pb_kernel(tc, t_bil, x_r, W_r, b_r, b_bil, out):
 
         keep_clock(4)
         transpose_x(0, x_sb[0][:].bitcast(F32), False)
-        keep_clock(1)
         w0 = transpose_tile(w_sb[0][:].bitcast(F32), False, 3)
         quantise_x(0)
         quantise_w(0, w0)
-        keep_clock(1)
         transpose_x(1, x_sb[1][:].bitcast(F32), False)
-        keep_clock(1)
         w1 = transpose_tile(w_sb[1][:].bitcast(F32), False, 3)
         quantise_x(1)
         quantise_w(1, w1)
@@ -270,46 +269,46 @@ def tile_bilinearpairedlayer_pb_kernel(tc, t_bil, x_r, W_r, b_r, b_bil, out):
         hidden(1, 0, 1)
         sorted_w3 = sort_words(w_sb[3], "w", 2)
         w2 = transpose_tile(sorted_w2, True, 3)
+        sort_t(0, 0)
         hidden(0, 2, 3)
         hidden(1, 2, 3)
-        sort_t(0, 0)
+        sort_t(0, 1)
         w3 = transpose_tile(sorted_w3, True, 3)
         quantise_w(2, w2)
-        sort_t(0, 1)
+        sort_t(0, 2)
         quantise_hidden(0, 0, on_vector)
         quantise_w(3, w3)
         hidden(0, 4, 5)
         hidden(1, 4, 5)
-        sort_t(0, 2)
         transpose_t(0, 0)
         transpose_t(0, 1)
         quantise_hidden(1, 0, on_vector)
         sort_t(0, 3)
+        sort_t(1, 0)
         hidden(0, 6, 7)
         quantise_t(0, 0, grouped[0, 0])
         transpose_t(0, 2)
         transpose_t(0, 3)
-        sort_t(1, 0)
-        sort_t(1, 1)
         quantise_t(0, 1, grouped[0, 1])
-        hidden(1, 6, 7)
         quantise_hidden(0, 1, on_vector)
+        sort_t(1, 1)
+        hidden(1, 6, 7)
+        scores(0, 0)
+        quantise_t(0, 2, grouped[0, 2])
         transpose_t(1, 0)
         transpose_t(1, 1)
-        quantise_t(0, 2, grouped[0, 2])
-        scores(0, 0, "VS")
         quantise_t(0, 3, grouped[0, 3])
         quantise_hidden(1, 1, on_vector)
-        scores(0, 1, "VS")
-        scores(0, 2, "VS")
-        quantise_t(1, 0, grouped[1, 0])
+        scores(0, 1)
         transpose_t(1, 2)
+        quantise_t(1, 0, grouped[1, 0])
         quantise_t(1, 1, grouped[1, 1])
-        scores(0, 3)
+        scores(0, 2)
         transpose_t(1, 3)
-        scores(1, 0, "VS")
         quantise_t(1, 2, grouped[1, 2])
-        scores(1, 1)
+        scores(0, 3, "VS")
         quantise_t(1, 3, grouped[1, 3])
+        scores(1, 0, "SV")
+        scores(1, 1, "SV")
         scores(1, 2)
         scores(1, 3)

@@ -63,7 +63,7 @@ def tile_bilinearpairedlayer_pb_kernel(tc, t_bil, x_r, W_r, b_r, b_bil, out):
                 cols = slice(n * width, (n + 1) * width)
                 nc.sync.dma_start(out=w_sb[a][:, cols], in_=w_rows[a // 2, a % 2][:, cols])
 
-        load_x(0, 2)
+        load_x(0, 4)
         load_w(0, 2)
         load_x(1, 1)
         nc.sync.dma_start(out=b_r_bf[:], in_=b_r.rearrange("(g p t) -> p g t", p=P, t=PACK))
@@ -255,17 +255,17 @@ def tile_bilinearpairedlayer_pb_kernel(tc, t_bil, x_r, W_r, b_r, b_bil, out):
 
         on_vector = [nc.vector.tensor_copy, nc.vector.tensor_copy]
 
-        keep_clock(4)
+        keep_clock(3)
         transpose_x(0, x_sb[0][:].bitcast(F32), False)
         w0 = transpose_tile(w_sb[0][:].bitcast(F32), False, 3)
         quantise_x(0)
         quantise_w(0, w0)
         transpose_x(1, x_sb[1][:].bitcast(F32), False)
-        w1 = transpose_tile(w_sb[1][:].bitcast(F32), False, 3)
-        quantise_x(1)
-        quantise_w(1, w1)
-        sorted_w2 = sort_words(w_sb[2], "w", 2)
         hidden(0, 0, 1)
+        quantise_x(1)
+        w1 = transpose_tile(w_sb[1][:].bitcast(F32), False, 3)
+        sorted_w2 = sort_words(w_sb[2], "w", 2)
+        quantise_w(1, w1)
         hidden(1, 0, 1)
         sorted_w3 = sort_words(w_sb[3], "w", 2)
         w2 = transpose_tile(sorted_w2, True, 3)

@@ -139,8 +139,6 @@ def tile_bilinearpairedlayer_pb_kernel(tc, t_bil, x_r, W_r, b_r, b_bil, out):
         def quantise_x(b):
             grouped = x_grouped[b]
             group = P * PACK
-            nc.vector.memset(grouped[:, 0:PACK], 0.0)
-            nc.vector.memset(grouped[:, 6 * group - PACK : 6 * group], 0.0)
             nc.vector.tensor_copy(out=grouped[:, PACK:group], in_=grouped[:, 4 * group : 5 * group - PACK])
             nc.vector.tensor_copy(out=grouped[:, 5 * group : 6 * group - PACK], in_=grouped[:, group + PACK : 2 * group])
             for lo, hi in ((0, 4), (4, 6)):
@@ -241,6 +239,10 @@ def tile_bilinearpairedlayer_pb_kernel(tc, t_bil, x_r, W_r, b_r, b_bil, out):
             if not by_halves:
                 nc.sync.dma_start(out=out_rows, in_=result[:])
 
+        for b in range(BATCH):
+            nc.vector.memset(x_grouped[b][:, 0:PACK], 0.0)
+            nc.vector.memset(x_grouped[b][:, (GROUPS * P - 1) * PACK : GROUPS * P * PACK], 0.0)
+
         ctx.enter_context(tc.manual_schedule())
         in_order = {}
         grouped = {}
@@ -262,8 +264,9 @@ def tile_bilinearpairedlayer_pb_kernel(tc, t_bil, x_r, W_r, b_r, b_bil, out):
         quantise_w(0, w0)
         transpose_x(1, x_sb[1][:].bitcast(F32), False)
         hidden(0, 0, 1)
+        sorted_w1 = sort_words(w_sb[1], "w", 2)
         quantise_x(1)
-        w1 = transpose_tile(w_sb[1][:].bitcast(F32), False, 3)
+        w1 = transpose_tile(sorted_w1, True, 3)
         sorted_w2 = sort_words(w_sb[2], "w", 2)
         quantise_w(1, w1)
         hidden(1, 0, 1)
@@ -299,7 +302,7 @@ def tile_bilinearpairedlayer_pb_kernel(tc, t_bil, x_r, W_r, b_r, b_bil, out):
         transpose_t(1, 1)
         quantise_t(0, 3, grouped[0, 3])
         quantise_hidden(1, 1, on_vector)
-        scores(0, 1)
+        scores(0, 1, "VS")
         transpose_t(1, 2)
         quantise_t(1, 0, grouped[1, 0])
         quantise_t(1, 1, grouped[1, 1])
@@ -309,6 +312,6 @@ def tile_bilinearpairedlayer_pb_kernel(tc, t_bil, x_r, W_r, b_r, b_bil, out):
         scores(0, 3, "VS")
         quantise_t(1, 3, grouped[1, 3])
         scores(1, 0, "SV")
-        scores(1, 1, "SV")
+        scores(1, 1)
         scores(1, 2)
         scores(1, 3)

@@ -81,16 +81,16 @@ def tile_bilinearpairedlayer_pb_kernel(tc, t_bil, x_r, W_r, b_r, b_bil, out):
         zeros = keep.tile([P, POS], BF16)
         nc.vector.memset(zeros[:], 0.0)
 
-        x_grouped = [keep.tile([P, GROUPS * P * PACK], BF16, name="x_grouped%d" % b, align_bytes=64) for b in range(BATCH)]
-        x_codes = [keep.tile([P, GROUPS * P], U32, name="x_codes%d" % b, align_bytes=64) for b in range(BATCH)]
-        x_scales = [keep.tile([P, GROUPS * P], U8, name="x_scales%d" % b, align_bytes=64) for b in range(BATCH)]
-        w_codes = keep.tile([P, TAPS * HID], U32, align_bytes=64)
-        w_scales = keep.tile([P, TAPS * HID], U8, align_bytes=64)
-        t_codes = [keep.tile([P, NOUT * HID_PASSES * POS], U32, name="t_codes%d" % b, align_bytes=64) for b in range(BATCH)]
-        t_scales = [keep.tile([P, NOUT * HID_PASSES * POS], U8, name="t_scales%d" % b, align_bytes=64) for b in range(BATCH)]
+        x_grouped = [keep.tile([P, GROUPS * P * PACK], BF16, name="x_grouped%d" % b, align_bytes=256) for b in range(BATCH)]
+        x_codes = [keep.tile([P, GROUPS * P], U32, name="x_codes%d" % b, align_bytes=256) for b in range(BATCH)]
+        x_scales = [keep.tile([P, GROUPS * P], U8, name="x_scales%d" % b, align_bytes=256) for b in range(BATCH)]
+        w_codes = keep.tile([P, TAPS * HID], U32, align_bytes=256)
+        w_scales = keep.tile([P, TAPS * HID], U8, align_bytes=256)
+        t_codes = [keep.tile([P, NOUT * HID_PASSES * POS], U32, name="t_codes%d" % b, align_bytes=256) for b in range(BATCH)]
+        t_scales = [keep.tile([P, NOUT * HID_PASSES * POS], U8, name="t_scales%d" % b, align_bytes=256) for b in range(BATCH)]
         h_rows = [[keep.tile([P, PACK, POS], BF16, name="h_rows%d_%d" % (b, g)) for g in range(HID_PASSES)] for b in range(BATCH)]
-        h_codes = [[keep.tile([P, POS], U32, name="h_codes%d_%d" % (b, g), align_bytes=64) for g in range(HID_PASSES)] for b in range(BATCH)]
-        h_scales = [[keep.tile([P, POS], U8, name="h_scales%d_%d" % (b, g), align_bytes=64) for g in range(HID_PASSES)] for b in range(BATCH)]
+        h_codes = [[keep.tile([P, POS], U32, name="h_codes%d_%d" % (b, g), align_bytes=256) for g in range(HID_PASSES)] for b in range(BATCH)]
+        h_scales = [[keep.tile([P, POS], U8, name="h_scales%d_%d" % (b, g), align_bytes=256) for g in range(HID_PASSES)] for b in range(BATCH)]
 
         def sort_words(src, tag, bufs):
             in_order = work.tile([P, src[:].shape[1] // 2], F32, name="in_order_" + tag, tag="in_order_" + tag, bufs=bufs)
@@ -117,7 +117,7 @@ def tile_bilinearpairedlayer_pb_kernel(tc, t_bil, x_r, W_r, b_r, b_bil, out):
 
         def transpose_tile(words, is_sorted, units):
             unit_elems = UNIT_COLS * PACK
-            grouped = work.tile([P, units * unit_elems], BF16, name="grouped%d" % units, tag="grouped%d" % units, bufs=GROUPED_BUFS[units], align_bytes=64)
+            grouped = work.tile([P, units * unit_elems], BF16, name="grouped%d" % units, tag="grouped%d" % units, bufs=GROUPED_BUFS[units], align_bytes=256)
             for unit in range(units):
                 transpose_unit(words, is_sorted, unit, nc.scalar.copy, grouped[:, unit * unit_elems : (unit + 1) * unit_elems])
             return grouped
@@ -179,7 +179,7 @@ def tile_bilinearpairedlayer_pb_kernel(tc, t_bil, x_r, W_r, b_r, b_bil, out):
                 )
 
         def quantise_hidden(b, g, copies):
-            grouped = work.tile([P, POS * PACK], BF16, tag="h_grouped", bufs=2, align_bytes=64)
+            grouped = work.tile([P, POS * PACK], BF16, tag="h_grouped", bufs=2, align_bytes=256)
             for half in range(2):
                 copies[half](
                     out=grouped[:, half * HALF_POS * PACK : (half + 1) * HALF_POS * PACK].rearrange(

from contextlib import ExitStack

import concourse.mybir as mybir
from concourse.masks import make_identity

BF16 = mybir.dt.bfloat16
F32 = mybir.dt.float32
U32 = mybir.dt.uint32
U8 = mybir.dt.uint8
FP8X4 = mybir.dt.float8_e4m3fn_x4
RELU = mybir.ActivationFunctionType.Relu
IDENTITY = mybir.ActivationFunctionType.Identity
ADD = mybir.AluOpType.add

BATCH, POS, FEAT, TAPS, HID, NOUT = 2, 512, 512, 3, 1024, 2
GROUPED_BUFS = {2: 4, 3: 2}
FLOPS = 2 * BATCH * POS * TAPS * FEAT * HID + 2 * BATCH * POS * NOUT * POS * HID

P = 128
PACK = 4
K_PASS = P * PACK
HALVES = 2
PASS_WORDS = HALVES * P
UNIT_BLOCKS = 2
UNIT_COLS = UNIT_BLOCKS * P
STRIDE = POS // P
GROUPS = STRIDE + 2
TAP_SHIFT = (0, 1, -1)
W_TILES = HID // (2 * P)
HID_PASSES = HID // K_PASS
POS_TILES = POS // P
HALF_POS = POS // 2


def tile_bilinearpairedlayer_pb_kernel(tc, t_bil, x_r, W_r, b_r, b_bil, out):
    nc = tc.nc
    with ExitStack() as ctx:
        keep = ctx.enter_context(tc.tile_pool(name="keep", bufs=1))
        work = ctx.enter_context(tc.tile_pool(name="work", bufs=4))
        psum = ctx.enter_context(tc.psum_pool(name="psum", bufs=8))

        b_r_bf = keep.tile([P, HID_PASSES, PACK], BF16)
        b_bil_bf = keep.tile([P, NOUT], BF16)

        x_sb = [keep.tile([P, STRIDE * FEAT], BF16, name="x_sb%d" % b) for b in range(BATCH)]
        w_sb = [keep.tile([P, 2 * TAPS * FEAT], BF16, name="w_sb%d" % a) for a in range(W_TILES)]
        t_sb = [
            [keep.tile([P, NOUT * HID], BF16, name="t_sb%d_%d" % (b, c)) for c in range(POS_TILES)]
            for b in range(BATCH)
        ]
        w_rows = W_r.rearrange("(g p h e) c -> g h p (e c)", p=P, h=2, e=2)

        def load_x(b, pieces):
            x_rows = x_r[b].rearrange("(q r) f -> q (r f)", r=STRIDE)
            width = STRIDE * FEAT // pieces
            for n in range(pieces):
                cols = slice(n * width, (n + 1) * width)
                nc.sync.dma_start(out=x_sb[b][:, cols], in_=x_rows[:, cols])

        def load_w(a, pieces):
            width = 2 * TAPS * FEAT // pieces
            for n in range(pieces):
                cols = slice(n * width, (n + 1) * width)
                nc.sync.dma_start(out=w_sb[a][:, cols], in_=w_rows[a // 2, a % 2][:, cols])

        load_x(0, 4)
        load_w(0, 2)
        load_x(1, 1)
        nc.sync.dma_start(out=b_r_bf[:], in_=b_r.rearrange("(g p t) -> p g t", p=P, t=PACK))
        for a in range(1, W_TILES):
            load_w(a, 1)
        for b in range(BATCH):
            t_rows = t_bil[b].rearrange("(c p) k g -> c p (k g)", p=P)
            for c in range(POS_TILES):
                nc.sync.dma_start(out=t_sb[b][c][:], in_=t_rows[c])

        nc.sync.dma_start(out=b_bil_bf[:], in_=b_bil.partition_broadcast(P))

        ident = keep.tile([P, P], F32)
        make_identity(nc, ident[:])
        zeros = keep.tile([P, POS], BF16)
        nc.vector.memset(zeros[:], 0.0)

        x_grouped = [keep.tile([P, GROUPS * P * PACK], BF16, name="x_grouped%d" % b, align_bytes=256) for b in range(BATCH)]
        x_codes = [keep.tile([P, GROUPS * P], U32, name="x_codes%d" % b, align_bytes=256) for b in range(BATCH)]
        x_scales = [keep.tile([P, GROUPS * P], U8, name="x_scales%d" % b, align_bytes=256) for b in range(BATCH)]
        w_codes = keep.tile([P, TAPS * HID], U32, align_bytes=256)
        w_scales = keep.tile([P, TAPS * HID], U8, align_bytes=256)
        t_codes = [keep.tile([P, NOUT * HID_PASSES * POS], U32, name="t_codes%d" % b, align_bytes=256) for b in range(BATCH)]
        t_scales = [keep.tile([P, NOUT * HID_PASSES * POS], U8, name="t_scales%d" % b, align_bytes=256) for b in range(BATCH)]
        h_rows = [[keep.tile([P, PACK, POS], BF16, name="h_rows%d_%d" % (b, g)) for g in range(HID_PASSES)] for b in range(BATCH)]
        h_codes = [[keep.tile([P, POS], U32, name="h_codes%d_%d" % (b, g), align_bytes=256) for g in range(HID_PASSES)] for b in range(BATCH)]
        h_scales = [[keep.tile([P, POS], U8, name="h_scales%d_%d" % (b, g), align_bytes=256) for g in range(HID_PASSES)] for b in range(BATCH)]

        def sort_words(src, tag, bufs):
            in_order = work.tile([P, src[:].shape[1] // 2], F32, name="in_order_" + tag, tag="in_order_" + tag, bufs=bufs)
            nc.vector.tensor_copy(
                out=in_order[:].rearrange("p (n u w) -> p n u w", u=HALVES, w=P),
                in_=src[:].bitcast(F32).rearrange("p (n w u) -> p n u w", u=HALVES, w=P),
            )
            return in_order

        def transpose_unit(words, is_sorted, unit, copy, grouped):
            bank = psum.tile([P, HALVES, UNIT_COLS], F32, tag="bank")
            for blk in range(UNIT_BLOCKS):
                first = (unit * UNIT_BLOCKS + blk) * PASS_WORDS
                for u in range(HALVES):
                    if is_sorted:
                        half = words[:, first + u * P : first + (u + 1) * P]
                    else:
                        half = words[:, first + u : first + PASS_WORDS : HALVES]
                    nc.tensor.transpose(bank[:, u, blk * P : (blk + 1) * P], half, ident[:])
            copy(
                out=grouped.bitcast(F32).rearrange("p (c u) -> p c u", u=HALVES),
                in_=bank[:].rearrange("p u c -> p c u"),
            )

        def transpose_tile(words, is_sorted, units):
            unit_elems = UNIT_COLS * PACK
            grouped = work.tile([P, units * unit_elems], BF16, name="grouped%d" % units, tag="grouped%d" % units, bufs=GROUPED_BUFS[units], align_bytes=256)
            for unit in range(units):
                transpose_unit(words, is_sorted, unit, nc.scalar.copy, grouped[:, unit * unit_elems : (unit + 1) * unit_elems])
            return grouped

        def quantise_units(grouped, codes, scales, first_col, lo, hi):
            cols = slice(first_col + lo * UNIT_COLS, first_col + hi * UNIT_COLS)
            nc.vector.quantize_mx(
                out=codes[:, cols].bitcast(FP8X4),
                scales=scales[:, cols],
                in_=grouped[:, lo * UNIT_COLS * PACK : hi * UNIT_COLS * PACK],
            )

        def transpose_x(b, words, is_sorted):
            group = P * PACK
            for unit in range(STRIDE // UNIT_BLOCKS):
                first = (1 + unit * UNIT_BLOCKS) * group
                transpose_unit(words, is_sorted, unit, nc.scalar.copy, x_grouped[b][:, first : first + UNIT_BLOCKS * group])

        def quantise_x(b):
            grouped = x_grouped[b]
            group = P * PACK
            nc.vector.tensor_copy(out=grouped[:, PACK:group], in_=grouped[:, 4 * group : 5 * group - PACK])
            nc.vector.tensor_copy(out=grouped[:, 5 * group : 6 * group - PACK], in_=grouped[:, group + PACK : 2 * group])
            for lo, hi in ((0, 4), (4, 6)):
                nc.vector.quantize_mx(
                    out=x_codes[b][:, lo * P : hi * P].bitcast(FP8X4),
                    scales=x_scales[b][:, lo * P : hi * P],
                    in_=grouped[:, lo * group : hi * group],
                )

        def quantise_w(a, grouped):
            for lo, hi in ((0, 2), (2, 3)):
                quantise_units(grouped, w_codes, w_scales, a * TAPS * UNIT_COLS, lo, hi)

        def quantise_t(b, c, grouped):
            quantise_units(grouped, t_codes[b], t_scales[b], c * NOUT * UNIT_COLS, 0, 2)

        def hidden(b, *chunks):
            for chunk in chunks:
                acc = psum.tile([P, POS], F32, tag="bank")
                for tap in range(TAPS):
                    w_cols = slice((chunk * TAPS + tap) * P, (chunk * TAPS + tap + 1) * P)
                    x_cols = slice((1 + TAP_SHIFT[tap]) * P, (1 + TAP_SHIFT[tap]) * P + POS)
                    nc.tensor.matmul_mx(
                        out=acc[:],
                        lhsT=w_codes[:, w_cols].bitcast(FP8X4),
                        lhsT_scale=w_scales[:, w_cols],
                        rhs=x_codes[b][:, x_cols].bitcast(FP8X4),
                        rhs_scale=x_scales[b][:, x_cols],
                        start=(tap == 0),
                        stop=(tap == TAPS - 1),
                    )
                nc.scalar.activation(
                    out=h_rows[b][chunk // PACK][:, chunk % PACK, :].rearrange("p (q r) -> p q r", r=STRIDE),
                    in_=acc[:].rearrange("p (r q) -> p q r", r=STRIDE),
                    func=RELU,
                    bias=b_r_bf[:, chunk // PACK, chunk % PACK : chunk % PACK + 1],
                    scale=1.0,
                )

        def quantise_hidden(b, g, copies):
            grouped = work.tile([P, POS * PACK], BF16, tag="h_grouped", bufs=2, align_bytes=256)
            for half in range(2):
                copies[half](
                    out=grouped[:, half * HALF_POS * PACK : (half + 1) * HALF_POS * PACK].rearrange(
                        "p (c i t) -> p c t i", i=4, t=PACK
                    ),
                    in_=h_rows[b][g][:, :, half * HALF_POS : (half + 1) * HALF_POS].rearrange("p t (c i) -> p c t i", i=4),
                )
            for half in range(2):
                cols = slice(half * HALF_POS, (half + 1) * HALF_POS)
                nc.vector.quantize_mx(
                    out=h_codes[b][g][:, cols].bitcast(FP8X4),
                    scales=h_scales[b][g][:, cols],
                    in_=grouped[:, half * HALF_POS * PACK : (half + 1) * HALF_POS * PACK],
                )

        def keep_clock(count):
            bank = psum.tile([P, POS], F32, tag="bank")
            for n in range(count):
                nc.tensor.matmul(bank[:], zeros[:, 0:P], zeros[:], start=True, stop=True)

        def scores(b, c, engines="VV"):
            by_halves = engines != "VV" or (b == BATCH - 1 and c == POS_TILES - 1)
            out_rows = out[b].rearrange("(c p) j k -> c p (j k)", p=P)[c]
            result = work.tile([P, POS * NOUT], F32, tag="result", bufs=6)
            for half in range(2):
                bank = psum.tile([P, NOUT, HALF_POS], F32, tag="bank")
                h_cols = slice(half * HALF_POS, (half + 1) * HALF_POS)
                for k in range(NOUT):
                    for g in range(HID_PASSES):
                        t_first = ((c * NOUT + k) * HID_PASSES + g) * P
                        nc.tensor.matmul_mx(
                            out=bank[:, k, :],
                            lhsT=t_codes[b][:, t_first : t_first + P].bitcast(FP8X4),
                            lhsT_scale=t_scales[b][:, t_first : t_first + P],
                            rhs=h_codes[b][g][:, h_cols].bitcast(FP8X4),
                            rhs_scale=h_scales[b][g][:, h_cols],
                            start=(g == 0),
                            stop=(g == HID_PASSES - 1),
                        )
                out_cols = slice(half * HALF_POS * NOUT, (half + 1) * HALF_POS * NOUT)
                by_k = result[:, out_cols].rearrange("p (j k) -> p j k", k=NOUT)
                if engines[half] == "V":
                    nc.vector.tensor_tensor(
                        out=by_k,
                        in0=bank[:].rearrange("p k j -> p j k"),
                        in1=b_bil_bf[:].unsqueeze(1).to_broadcast([P, HALF_POS, NOUT]),
                        op=ADD,
                    )
                else:
                    for k in range(NOUT):
                        nc.scalar.activation(
                            out=by_k[:, :, k], in_=bank[:, k, :], func=IDENTITY, bias=b_bil_bf[:, k : k + 1], scale=1.0
                        )
                if by_halves:
                    queue = nc.scalar if engines[half] == "S" else nc.sync
                    queue.dma_start(out=out_rows[:, out_cols], in_=result[:, out_cols])
            if not by_halves:
                nc.sync.dma_start(out=out_rows, in_=result[:])

        for b in range(BATCH):
            nc.vector.memset(x_grouped[b][:, 0:PACK], 0.0)
            nc.vector.memset(x_grouped[b][:, (GROUPS * P - 1) * PACK : GROUPS * P * PACK], 0.0)

        ctx.enter_context(tc.manual_schedule())
        in_order = {}
        grouped = {}

        def sort_t(b, c):
            in_order[b, c] = sort_words(t_sb[b][c], "t", 4)

        def transpose_t(b, c):
            is_sorted = (b, c) in in_order
            words = in_order[b, c] if is_sorted else t_sb[b][c][:].bitcast(F32)
            grouped[b, c] = transpose_tile(words, is_sorted, 2)

        on_vector = [nc.vector.tensor_copy, nc.vector.tensor_copy]

        keep_clock(3)
        transpose_x(0, x_sb[0][:].bitcast(F32), False)
        w0 = transpose_tile(w_sb[0][:].bitcast(F32), False, 3)
        quantise_x(0)
        quantise_w(0, w0)
        transpose_x(1, x_sb[1][:].bitcast(F32), False)
        hidden(0, 0, 1)
        sorted_w1 = sort_words(w_sb[1], "w", 2)
        quantise_x(1)
        w1 = transpose_tile(sorted_w1, True, 3)
        sorted_w2 = sort_words(w_sb[2], "w", 2)
        quantise_w(1, w1)
        hidden(1, 0, 1)
        sorted_w3 = sort_words(w_sb[3], "w", 2)
        w2 = transpose_tile(sorted_w2, True, 3)
        sort_t(0, 0)
        hidden(0, 2, 3)
        hidden(1, 2, 3)
        sort_t(0, 1)
        w3 = transpose_tile(sorted_w3, True, 3)
        quantise_w(2, w2)
        sort_t(0, 2)
        quantise_hidden(0, 0, on_vector)
        quantise_w(3, w3)
        hidden(0, 4, 5)
        hidden(1, 4, 5)
        transpose_t(0, 0)
        transpose_t(0, 1)
        quantise_hidden(1, 0, on_vector)
        sort_t(0, 3)
        sort_t(1, 0)
        hidden(0, 6, 7)
        quantise_t(0, 0, grouped[0, 0])
        transpose_t(0, 2)
        transpose_t(0, 3)
        quantise_t(0, 1, grouped[0, 1])
        quantise_hidden(0, 1, on_vector)
        sort_t(1, 1)
        hidden(1, 6, 7)
        scores(0, 0)
        quantise_t(0, 2, grouped[0, 2])
        transpose_t(1, 0)
        transpose_t(1, 1)
        quantise_t(0, 3, grouped[0, 3])
        quantise_hidden(1, 1, on_vector)
        scores(0, 1, "VS")
        transpose_t(1, 2)
        quantise_t(1, 0, grouped[1, 0])
        quantise_t(1, 1, grouped[1, 1])
        scores(0, 2)
        transpose_t(1, 3)
        quantise_t(1, 2, grouped[1, 2])
        scores(0, 3, "VS")
        quantise_t(1, 3, grouped[1, 3])
        scores(1, 0, "SV")
        scores(1, 1)
        scores(1, 2)
        scores(1, 3)
